import numpy as np
import ml_dtypes


def mxq(x, axis, fmt="e4m3"):
    dtype, down = {"e4m3": (ml_dtypes.float8_e4m3fn, 7), "e5m2": (ml_dtypes.float8_e5m2, 14)}[fmt]
    v = np.moveaxis(np.asarray(x, np.float32).astype(ml_dtypes.bfloat16).astype(np.float64), axis, -1)
    blocks = v.reshape(v.shape[:-1] + (-1, 32))
    amax = np.abs(blocks).max(-1, keepdims=True)
    byte = np.maximum(np.where(amax > 0, np.frexp(amax)[1] - 1 + 127, 0) - down, 1)
    scale = np.exp2(byte - 127.0)
    codes = (blocks / scale).astype(np.float32).astype(dtype).astype(np.float64)
    return np.moveaxis((codes * scale).reshape(v.shape), -1, axis)


WIDE = False


def mx_kscale(k):
    if not WIDE:
        return np.ones(k)
    levels = np.array([10, -10, 5, -5, 0])
    if k % 512:
        return np.exp2(np.random.permutation(np.resize(levels, k // 32))).repeat(32)
    a = np.empty((k // 512, 16))
    for p in range(k // 512):
        a[p, :8] = np.random.permutation(np.resize(levels, 8))
        for g in range(8):
            far = levels[np.abs(levels - a[p, g]) >= 10]
            a[p, g + 8] = far[np.random.randint(len(far))]
    return np.exp2(a.ravel()).repeat(32)


BF16 = ml_dtypes.bfloat16


def bf(x):
    return np.asarray(x, np.float32).astype(BF16)


def f64(x):
    return np.asarray(x).astype(np.float64)


B, DIN, H1, H2, N, I, K, O = 1024, 2048, 1024, 512, 32, 16, 256, 16
NI = N * I
KO = K * O
SQ_EPS = 1e-8


def squash(t):
    sq = np.sum(t * t, axis=-1, keepdims=True)
    return (sq / (1.0 + sq)) * t / np.sqrt(sq + SQ_EPS)


def setup_inputs():
    s = mx_kscale(NI).reshape(N, I)
    return {"p": bf(np.random.standard_normal((B, N, I)) * s),
            "Wr": bf(np.random.standard_normal((N, K, O, I)) * K / np.sqrt(NI * O) / s[:, None, None, :])}


def reference(p, Wr):
    c = 1.0 / K
    pf = f64(p).reshape(B, NI)
    wf = f64(Wr).transpose(0, 3, 1, 2).reshape(NI, KO)
    s = (mxq(pf, 1, "e4m3") @ mxq(wf, 0, "e4m3")).reshape(B, K, O) * c
    return squash(s)

@@ -1,0 +1,341 @@
+from contextlib import ExitStack
+
+import concourse.mybir as mybir
+from concourse.masks import make_identity
+
+F32 = mybir.dt.float32
+BF16 = mybir.dt.bfloat16
+U32 = mybir.dt.uint32
+U8 = mybir.dt.uint8
+FP8X4 = mybir.dt.float8_e4m3fn_x4
+ACT = mybir.ActivationFunctionType
+ALU = mybir.AluOpType
+
+P = 128
+B = 1024
+K = 512
+I = 16
+J = 256
+O = 16
+COLS = J * O
+B_TILES = B // P
+N_HALF = 16
+BANK = 512
+QUARTERS = BANK // P
+J_CHUNK = 64
+CHUNK = J_CHUNK * O
+N_CHUNKS = J // J_CHUNK
+O_LOW = 4
+O_HIGH = O // O_LOW
+J_BLOCK = P // O_LOW
+BLOCKS_PER_HIGH = J_CHUNK // J_BLOCK
+HIGH_PER_BANK = BANK // (J_CHUNK * O_LOW)
+
+GROUP_TILES = 2
+GROUP_BANKS = 4
+GROUP_J = GROUP_TILES * J_CHUNK
+GROUPS_PER_CHUNK = B_TILES // GROUP_TILES
+N_GROUPS = N_CHUNKS * GROUPS_PER_CHUNK
+LAG_SUMS = 1
+LAG_FACTOR = 2
+LAG_OUTPUT = 3
+
+COUPLING = 1.0 / 256.0
+SQ_EPS = 1e-8
+SHRINK = 2.0 ** -32
+
+FLOPS = 2 * B * K * COLS
+
+
+def tile_capsulenetwork_pb_kernel(tc, p, Wr, out):
+    nc = tc.nc
+    out_rows = out.rearrange("(r t) j o -> r t (j o)", t=B_TILES)
+
+    with ExitStack() as ctx:
+        keep = ctx.enter_context(tc.tile_pool(name="keep", bufs=1))
+        wload = ctx.enter_context(tc.tile_pool(name="wload", bufs=N_CHUNKS))
+        stage = ctx.enter_context(tc.tile_pool(name="stage", bufs=2))
+        work = ctx.enter_context(tc.tile_pool(name="work", bufs=3))
+        results = ctx.enter_context(tc.tile_pool(name="results", bufs=4))
+        psum_turn = ctx.enter_context(tc.psum_pool(name="psum_turn", bufs=2))
+        psum_norm = ctx.enter_context(tc.psum_pool(name="psum_norm", bufs=2))
+        psum_sums = ctx.enter_context(tc.psum_pool(name="psum_sums", bufs=1))
+        psum_out = ctx.enter_context(tc.psum_pool(name="psum_out", bufs=3))
+
+        def load_w_chunk(c):
+            w_raw = wload.tile([P, N_HALF, O * I], BF16)
+            for u in range(2):
+                nc.sync.dma_start(
+                    out=w_raw[u:P:2, :, :],
+                    in_=Wr[
+                        u : 2 * N_HALF : 2, c * J_CHUNK : (c + 1) * J_CHUNK, :, :
+                    ].rearrange("n j o i -> j n (o i)"),
+                )
+            return w_raw
+
+        w_raws = [load_w_chunk(0)]
+        p_raw = keep.tile([P, B_TILES * K], BF16)
+        nc.sync.dma_start(out=p_raw[:], in_=p.rearrange("(r t) n i -> r (t n i)", t=B_TILES))
+        w_raws.extend([load_w_chunk(c) for c in range(1, N_CHUNKS)])
+
+        shrink_col = keep.tile([P, 1], F32)
+        nc.vector.memset(shrink_col[:], SHRINK)
+        table_warmer = keep.tile([P, 1], F32)
+        nc.scalar.activation(out=table_warmer[:], in_=shrink_col[:], func=ACT.Abs_reciprocal_sqrt)
+
+        ident = keep.tile([P, P], F32)
+        make_identity(nc, ident[:])
+
+        p_codes = keep.tile([P, B_TILES * P], U32, align_bytes=64)
+        p_scales = keep.tile([P, B_TILES * P], U8, align_bytes=64)
+        w_codes = keep.tile([P, COLS], U32, align_bytes=64)
+        w_scales = keep.tile([P, COLS], U8, align_bytes=64)
+
+        def copy_out_of_psum(out_view, in_view, on_vector):
+            if on_vector:
+                nc.vector.tensor_copy(out=out_view, in_=in_view)
+            else:
+                nc.scalar.copy(out=out_view, in_=in_view)
+
+        w_sorted = {}
+        w_grouped = {}
+
+        def sort_w(c):
+            sorted_tile = stage.tile([P, O * N_HALF * I], BF16)
+            nc.vector.tensor_copy(
+                out=sorted_tile[:].rearrange("q (o n i) -> q o n i", o=O, i=I),
+                in_=w_raws[c][:].rearrange("q n (o i) -> q o n i", i=I),
+            )
+            w_sorted[c] = sorted_tile
+            grouped_tile = stage.tile([P, CHUNK * 4], BF16, align_bytes=64)
+            w_grouped[c] = grouped_tile
+
+        def turn_w(c, g, on_vector):
+            words = w_sorted[c][:].bitcast(F32)
+            turned = psum_turn.tile([P, BANK], F32)
+            for ol in range(O_LOW):
+                o = O_LOW * g + ol
+                nc.tensor.transpose(turned[:, ol * P : (ol + 1) * P], words[:, o * P : (o + 1) * P], ident[:])
+            copy_out_of_psum(
+                w_grouped[c][:].bitcast(F32)[:, g * BANK : (g + 1) * BANK].rearrange(
+                    "m (j l u) -> m j l u", l=O_LOW, u=2
+                ),
+                turned[:].rearrange("m (l j u) -> m j l u", l=O_LOW, u=2),
+                on_vector,
+            )
+
+        def quantise_w(c):
+            chunk_cols = slice(c * CHUNK, (c + 1) * CHUNK)
+            nc.vector.quantize_mx(
+                out=w_codes[:, chunk_cols].bitcast(FP8X4),
+                scales=w_scales[:, chunk_cols],
+                in_=w_grouped[c][:],
+            )
+
+        sort_w(0)
+        for g in range(O_HIGH):
+            turn_w(0, g, on_vector=(g % 2 == 1))
+        quantise_w(0)
+
+        p_sorted = keep.tile([P, B_TILES, 2, N_HALF, I], BF16)
+        p_by_half = p_raw[:].rearrange("r (t g u i) -> r t g u i", t=B_TILES, u=2, i=I)
+        for u in range(2):
+            nc.scalar.copy(out=p_sorted[:, :, u, :, :], in_=p_by_half[:, :, :, u, :])
+        p_words = p_sorted[:].rearrange("r t u g i -> r (t u g i)").bitcast(F32)
+        p_grouped = keep.tile([P, B_TILES * P * 4], BF16, align_bytes=64)
+        p_grouped_words = p_grouped[:].bitcast(F32)
+
+        def quantise_p(pair):
+            nc.vector.quantize_mx(
+                out=p_codes[:, pair * 2 * P : (pair + 1) * 2 * P].bitcast(FP8X4),
+                scales=p_scales[:, pair * 2 * P : (pair + 1) * 2 * P],
+                in_=p_grouped[:, pair * 2 * P * 4 : (pair + 1) * 2 * P * 4],
+            )
+
+        for pair in range(B_TILES // 2):
+            turned = psum_turn.tile([P, BANK], F32)
+            for tu in range(QUARTERS):
+                first_word = (pair * QUARTERS + tu) * P
+                nc.tensor.transpose(
+                    turned[:, tu * P : (tu + 1) * P], p_words[:, first_word : first_word + P], ident[:]
+                )
+            copy_out_of_psum(
+                p_grouped_words[:, pair * BANK : (pair + 1) * BANK].rearrange(
+                    "m (t r u) -> m t r u", t=2, u=2
+                ),
+                turned[:].rearrange("m (t u r) -> m t r u", t=2, u=2),
+                on_vector=(pair % 2 == 1),
+            )
+            if pair >= 1:
+                quantise_p(pair - 1)
+        quantise_p(B_TILES // 2 - 1)
+
+        squares = {}
+        partial_sums = {}
+        lengths = {}
+        one_plus_sq = {}
+        denom_sq = {}
+        seeds = {}
+        factors = {}
+        result = {}
+
+        def square_bank(group, oh):
+            if oh == 0:
+                squares_tile = work.tile([P, O_HIGH * BLOCKS_PER_HIGH, GROUP_TILES, P], F32)
+                squares[group] = squares_tile
+            first_row = (group % GROUPS_PER_CHUNK) * GROUP_TILES * P
+            acc = psum_norm.tile([P, BLOCKS_PER_HIGH, GROUP_TILES * P], F32)
+            for block in range(BLOCKS_PER_HIGH):
+                first_col = (group // GROUPS_PER_CHUNK) * CHUNK + (oh * BLOCKS_PER_HIGH + block) * P
+                nc.tensor.matmul_mx(
+                    out=acc[:, block, :],
+                    lhsT=w_codes[:, first_col : first_col + P].bitcast(FP8X4),
+                    lhsT_scale=w_scales[:, first_col : first_col + P],
+                    rhs=p_codes[:, first_row : first_row + GROUP_TILES * P].bitcast(FP8X4),
+                    rhs_scale=p_scales[:, first_row : first_row + GROUP_TILES * P],
+                    start=True,
+                    stop=True,
+                )
+            nc.scalar.activation(
+                out=squares[group][:, oh * BLOCKS_PER_HIGH : (oh + 1) * BLOCKS_PER_HIGH, :, :].rearrange(
+                    "q b t r -> q b (t r)"
+                ),
+                in_=acc[:],
+                func=ACT.Square,
+                scale=COUPLING,
+            )
+
+        def sum_squares(group):
+            sums = psum_sums.tile([P, GROUP_TILES, BLOCKS_PER_HIGH, P], F32)
+            for tile_in_group in range(GROUP_TILES):
+                for block in range(BLOCKS_PER_HIGH):
+                    for oh in range(O_HIGH):
+                        nc.tensor.matmul(
+                            out=sums[:, tile_in_group, block, :],
+                            lhsT=squares[group][:, oh * BLOCKS_PER_HIGH + block, tile_in_group, :],
+                            rhs=ident[:],
+                            is_transpose=True,
+                            start=(oh == 0),
+                            stop=(oh == O_HIGH - 1),
+                        )
+            partial_sums[group] = sums
+
+        def factor_lengths(group):
+            q = work.tile([P, GROUP_J], F32)
+            nc.vector.tensor_reduce(
+                out=q[:],
+                in_=partial_sums[group][:].rearrange("r t b (j l) -> r (t b j) l", l=O_LOW),
+                axis=mybir.AxisListType.X,
+                op=ALU.add,
+            )
+            lengths[group] = q
+
+        def factor_one_plus_q(group):
+            one_plus_q_sq = work.tile([P, GROUP_J], F32)
+            nc.scalar.activation(
+                out=one_plus_q_sq[:],
+                in_=lengths[group][:],
+                func=ACT.Square,
+                scale=SHRINK,
+                bias=shrink_col[:],
+            )
+            one_plus_sq[group] = one_plus_q_sq
+
+        def factor_denominator(group):
+            x = work.tile([P, GROUP_J], F32)
+            nc.vector.scalar_tensor_tensor(
+                out=x[:],
+                in0=lengths[group][:],
+                scalar=SQ_EPS,
+                in1=one_plus_sq[group][:],
+                op0=ALU.add,
+                op1=ALU.mult,
+            )
+            denom_sq[group] = x
+
+        def factor_seed(group):
+            y = work.tile([P, GROUP_J], F32)
+            nc.scalar.activation(out=y[:], in_=denom_sq[group][:], func=ACT.Abs_reciprocal_sqrt)
+            y_sq = work.tile([P, GROUP_J], F32)
+            nc.scalar.activation(out=y_sq[:], in_=y[:], func=ACT.Square)
+            seeds[group] = (y, y_sq)
+
+        def factor_newton(group):
+            y, y_sq = seeds[group]
+            x_y_sq = work.tile([P, GROUP_J], F32)
+            nc.vector.tensor_tensor(out=x_y_sq[:], in0=denom_sq[group][:], in1=y_sq[:], op=ALU.mult)
+            rough = work.tile([P, GROUP_J], F32)
+            nc.vector.scalar_tensor_tensor(
+                out=rough[:],
+                in0=lengths[group][:],
+                scalar=-0.5 * SHRINK * COUPLING,
+                in1=y[:],
+                op0=ALU.mult,
+                op1=ALU.mult,
+            )
+            factor = work.tile([P, GROUP_J], F32)
+            nc.vector.scalar_tensor_tensor(
+                out=factor[:], in0=x_y_sq[:], scalar=3.0, in1=rough[:], op0=ALU.subtract, op1=ALU.mult
+            )
+            factors[group] = factor
+
+        def output_bank(group, k):
+            tile_in_group = k // 2
+            half = k % 2
+            t = GROUP_TILES * (group % GROUPS_PER_CHUNK) + tile_in_group
+            c = group // GROUPS_PER_CHUNK
+            first_col = c * CHUNK + half * BANK
+            acc = psum_out.tile([P, HIGH_PER_BANK, J_CHUNK, O_LOW], F32)
+            nc.tensor.matmul_mx(
+                out=acc[:].rearrange("r h j l -> r (h j l)"),
+                lhsT=p_codes[:, t * P : (t + 1) * P].bitcast(FP8X4),
+                lhsT_scale=p_scales[:, t * P : (t + 1) * P],
+                rhs=w_codes[:, first_col : first_col + BANK].bitcast(FP8X4),
+                rhs_scale=w_scales[:, first_col : first_col + BANK],
+                start=True,
+                stop=True,
+            )
+            if half == 0:
+                result_tile = results.tile([P, J_CHUNK, O_HIGH, O_LOW], F32)
+                result[group] = result_tile
+            nc.vector.tensor_tensor(
+                out=result[group][:, :, half * HIGH_PER_BANK : (half + 1) * HIGH_PER_BANK, :],
+                in0=acc[:].rearrange("r h j l -> r j h l"),
+                in1=factors[group][:, tile_in_group * J_CHUNK : (tile_in_group + 1) * J_CHUNK]
+                .unsqueeze(2)
+                .unsqueeze(3)
+                .to_broadcast([P, J_CHUNK, HIGH_PER_BANK, O_LOW]),
+                op=ALU.mult,
+            )
+            if half == 1:
+                nc.sync.dma_start(
+                    out=out_rows[:, t, c * CHUNK : (c + 1) * CHUNK],
+                    in_=result[group][:].rearrange("r j h l -> r (j h l)"),
+                )
+
+        for i in range(N_GROUPS + LAG_OUTPUT):
+            prepare = 1 <= i < N_CHUNKS
+            if prepare:
+                sort_w(i)
+            for k in range(GROUP_BANKS):
+                if i < N_GROUPS:
+                    square_bank(i, k)
+                if k == 0 and i >= LAG_OUTPUT:
+                    factor_newton(i - LAG_OUTPUT)
+                if 0 <= i - LAG_FACTOR < N_GROUPS:
+                    if k == 0:
+                        factor_lengths(i - LAG_FACTOR)
+                    if k == 1:
+                        factor_one_plus_q(i - LAG_FACTOR)
+                    if k == 2:
+                        factor_denominator(i - LAG_FACTOR)
+                    if k == 3:
+                        factor_seed(i - LAG_FACTOR)
+                if i >= LAG_OUTPUT:
+                    output_bank(i - LAG_OUTPUT, k)
+                if prepare:
+                    turn_w(i, k, on_vector=(i < LAG_OUTPUT))
+            if prepare:
+                quantise_w(i)
+            if 0 <= i - LAG_SUMS < N_GROUPS:
+                sum_squares(i - LAG_SUMS)

@@ -14,31 +14,28 @@ ALU = mybir.AluOpType
 P = 128
 B = 1024
 K = 512
+N_CAPS = 32
 I = 16
 J = 256
 O = 16
 COLS = J * O
 B_TILES = B // P
-N_HALF = 16
+G = N_CAPS // 2
 BANK = 512
-QUARTERS = BANK // P
-J_CHUNK = 64
+J_CHUNK = 128
 CHUNK = J_CHUNK * O
 N_CHUNKS = J // J_CHUNK
-O_LOW = 4
-O_HIGH = O // O_LOW
-J_BLOCK = P // O_LOW
-BLOCKS_PER_HIGH = J_CHUNK // J_BLOCK
-HIGH_PER_BANK = BANK // (J_CHUNK * O_LOW)
+O_TURN = 2
+O_QUANT = 4
+O_OUT = BANK // J_CHUNK
 
 GROUP_TILES = 2
-GROUP_BANKS = 4
-GROUP_J = GROUP_TILES * J_CHUNK
+GROUP_ROWS = GROUP_TILES * P
+O_NORM = BANK // GROUP_ROWS
+GROUP_BANKS = 8
+GROUP_Q = GROUP_TILES * J_CHUNK
 GROUPS_PER_CHUNK = B_TILES // GROUP_TILES
 N_GROUPS = N_CHUNKS * GROUPS_PER_CHUNK
-LAG_SUMS = 1
-LAG_FACTOR = 2
-LAG_OUTPUT = 3
 
 COUPLING = 1.0 / 256.0
 SQ_EPS = 1e-8
@@ -53,30 +50,39 @@ def tile_capsulenetwork_pb_kernel(tc, p, Wr, out):
 
     with ExitStack() as ctx:
         keep = ctx.enter_context(tc.tile_pool(name="keep", bufs=1))
-        wload = ctx.enter_context(tc.tile_pool(name="wload", bufs=N_CHUNKS))
         stage = ctx.enter_context(tc.tile_pool(name="stage", bufs=2))
+        quarters = ctx.enter_context(tc.tile_pool(name="quarters", bufs=4))
+        squares_pool = ctx.enter_context(tc.tile_pool(name="squares_pool", bufs=6))
+        pair_pool = ctx.enter_context(tc.tile_pool(name="pair_pool", bufs=3))
         work = ctx.enter_context(tc.tile_pool(name="work", bufs=3))
         results = ctx.enter_context(tc.tile_pool(name="results", bufs=4))
-        psum_turn = ctx.enter_context(tc.psum_pool(name="psum_turn", bufs=2))
-        psum_norm = ctx.enter_context(tc.psum_pool(name="psum_norm", bufs=2))
+        psum_banks = ctx.enter_context(tc.psum_pool(name="psum_banks", bufs=7))
         psum_sums = ctx.enter_context(tc.psum_pool(name="psum_sums", bufs=1))
-        psum_out = ctx.enter_context(tc.psum_pool(name="psum_out", bufs=3))
 
-        def load_w_chunk(c):
-            w_raw = wload.tile([P, N_HALF, O * I], BF16)
-            for u in range(2):
+        p_raw = keep.tile([P, B_TILES, K], BF16)
+
+        def load_p(pair):
+            tiles = slice(2 * pair, 2 * pair + 2)
+            nc.sync.dma_start(
+                out=p_raw[:, tiles, :], in_=p.rearrange("(r t) n i -> r t (n i)", t=B_TILES)[:, tiles, :]
+            )
+
+        load_p(0)
+        w_raws = []
+        PIECES = 4
+        N_PIECE = N_CAPS // PIECES
+        for c in range(N_CHUNKS):
+            w_raw = stage.tile([P, N_CAPS, O * I], BF16)
+            w_raws.append(w_raw)
+            for piece in range(PIECES):
+                caps = slice(piece * N_PIECE, (piece + 1) * N_PIECE)
                 nc.sync.dma_start(
-                    out=w_raw[u:P:2, :, :],
-                    in_=Wr[
-                        u : 2 * N_HALF : 2, c * J_CHUNK : (c + 1) * J_CHUNK, :, :
-                    ].rearrange("n j o i -> j n (o i)"),
+                    out=w_raw[:, caps, :],
+                    in_=Wr[caps, c * J_CHUNK : (c + 1) * J_CHUNK, :, :].rearrange("n j o i -> j n (o i)"),
                 )
-            return w_raw
-
-        w_raws = [load_w_chunk(0)]
-        p_raw = keep.tile([P, B_TILES * K], BF16)
-        nc.sync.dma_start(out=p_raw[:], in_=p.rearrange("(r t) n i -> r (t n i)", t=B_TILES))
-        w_raws.extend([load_w_chunk(c) for c in range(1, N_CHUNKS)])
+            if c == 0:
+                for pair in range(1, B_TILES // 2):
+                    load_p(pair)
 
         shrink_col = keep.tile([P, 1], F32)
         nc.vector.memset(shrink_col[:], SHRINK)
@@ -98,49 +104,60 @@ def tile_capsulenetwork_pb_kernel(tc, p, Wr, out):
                 nc.scalar.copy(out=out_view, in_=in_view)
 
         w_sorted = {}
-        w_grouped = {}
+        w_quarters = {}
 
-        def sort_w(c):
-            sorted_tile = stage.tile([P, O * N_HALF * I], BF16)
-            nc.vector.tensor_copy(
-                out=sorted_tile[:].rearrange("q (o n i) -> q o n i", o=O, i=I),
-                in_=w_raws[c][:].rearrange("q n (o i) -> q o n i", i=I),
-            )
-            w_sorted[c] = sorted_tile
-            grouped_tile = stage.tile([P, CHUNK * 4], BF16, align_bytes=64)
-            w_grouped[c] = grouped_tile
+        def sort_w(c, piece):
+            if piece == 0:
+                sorted_tile = stage.tile([P, O, 2, G, I], BF16)
+                w_sorted[c] = sorted_tile
+            by_half = w_raws[c][:].rearrange("q (g u) (o i) -> q u o g i", u=2, i=I)
+            pairs = slice(piece * N_PIECE // 2, (piece + 1) * N_PIECE // 2)
+            for u in range(2):
+                nc.vector.tensor_copy(out=w_sorted[c][:, :, u, pairs, :], in_=by_half[:, u, :, pairs, :])
 
-        def turn_w(c, g, on_vector):
-            words = w_sorted[c][:].bitcast(F32)
-            turned = psum_turn.tile([P, BANK], F32)
-            for ol in range(O_LOW):
-                o = O_LOW * g + ol
-                nc.tensor.transpose(turned[:, ol * P : (ol + 1) * P], words[:, o * P : (o + 1) * P], ident[:])
+        turned_banks = {}
+
+        def turn_w(c, bank):
+            words = w_sorted[c][:].rearrange("q o u g i -> q (o u g i)").bitcast(F32)
+            turned = psum_banks.tile([P, BANK], F32, tag="bank")
+            for ou in range(O_TURN * 2):
+                first_word = (bank * O_TURN * 2 + ou) * P
+                nc.tensor.transpose(
+                    turned[:, ou * P : (ou + 1) * P], words[:, first_word : first_word + P], ident[:]
+                )
+            turned_banks[(c, bank)] = turned
+
+        def group_w(c, bank, on_vector):
+            turned = turned_banks[(c, bank)]
+            half = bank % 2
+            if half == 0:
+                quarter = quarters.tile([P, O_QUANT * J_CHUNK * 4], BF16, align_bytes=64)
+                w_quarters[(c, bank // 2)] = quarter
             copy_out_of_psum(
-                w_grouped[c][:].bitcast(F32)[:, g * BANK : (g + 1) * BANK].rearrange(
-                    "m (j l u) -> m j l u", l=O_LOW, u=2
+                w_quarters[(c, bank // 2)][:].bitcast(F32)[:, half * BANK : (half + 1) * BANK].rearrange(
+                    "m (o j u) -> m o j u", o=O_TURN, u=2
                 ),
-                turned[:].rearrange("m (l j u) -> m j l u", l=O_LOW, u=2),
+                turned[:].rearrange("m (o u j) -> m o j u", o=O_TURN, u=2),
                 on_vector,
             )
 
-        def quantise_w(c):
-            chunk_cols = slice(c * CHUNK, (c + 1) * CHUNK)
+        def quantise_w(c, quarter):
+            first_col = c * CHUNK + quarter * O_QUANT * J_CHUNK
+            cols = slice(first_col, first_col + O_QUANT * J_CHUNK)
             nc.vector.quantize_mx(
-                out=w_codes[:, chunk_cols].bitcast(FP8X4),
-                scales=w_scales[:, chunk_cols],
-                in_=w_grouped[c][:],
+                out=w_codes[:, cols].bitcast(FP8X4),
+                scales=w_scales[:, cols],
+                in_=w_quarters[(c, quarter)][:],
             )
 
-        sort_w(0)
-        for g in range(O_HIGH):
-            turn_w(0, g, on_vector=(g % 2 == 1))
-        quantise_w(0)
+        p_sorted = keep.tile([P, B_TILES, 2, G, I], BF16)
+        p_by_half = p_raw[:].rearrange("r t (g u i) -> r t g u i", u=2, i=I)
 
-        p_sorted = keep.tile([P, B_TILES, 2, N_HALF, I], BF16)
-        p_by_half = p_raw[:].rearrange("r (t g u i) -> r t g u i", t=B_TILES, u=2, i=I)
-        for u in range(2):
-            nc.scalar.copy(out=p_sorted[:, :, u, :, :], in_=p_by_half[:, :, :, u, :])
+        def sort_p(pair):
+            tiles = slice(2 * pair, 2 * pair + 2)
+            for u in range(2):
+                nc.vector.tensor_copy(out=p_sorted[:, tiles, u, :, :], in_=p_by_half[:, tiles, :, u, :])
+
         p_words = p_sorted[:].rearrange("r t u g i -> r (t u g i)").bitcast(F32)
         p_grouped = keep.tile([P, B_TILES * P * 4], BF16, align_bytes=64)
         p_grouped_words = p_grouped[:].bitcast(F32)
@@ -152,97 +169,89 @@ def tile_capsulenetwork_pb_kernel(tc, p, Wr, out):
                 in_=p_grouped[:, pair * 2 * P * 4 : (pair + 1) * 2 * P * 4],
             )
 
-        for pair in range(B_TILES // 2):
-            turned = psum_turn.tile([P, BANK], F32)
-            for tu in range(QUARTERS):
-                first_word = (pair * QUARTERS + tu) * P
+        def turn_p(pair):
+            turned = psum_banks.tile([P, BANK], F32, tag="bank")
+            for tu in range(4):
+                first_word = (pair * 4 + tu) * P
                 nc.tensor.transpose(
                     turned[:, tu * P : (tu + 1) * P], p_words[:, first_word : first_word + P], ident[:]
                 )
-            copy_out_of_psum(
-                p_grouped_words[:, pair * BANK : (pair + 1) * BANK].rearrange(
-                    "m (t r u) -> m t r u", t=2, u=2
-                ),
-                turned[:].rearrange("m (t u r) -> m t r u", t=2, u=2),
-                on_vector=(pair % 2 == 1),
-            )
-            if pair >= 1:
-                quantise_p(pair - 1)
-        quantise_p(B_TILES // 2 - 1)
+            turned_p[pair] = turned
 
-        squares = {}
-        partial_sums = {}
+        turned_p = {}
+
+        def group_p(pair, on_vector):
+            turned = turned_p[pair]
+            copy_out_of_psum(
+                p_grouped_words[:, pair * BANK : (pair + 1) * BANK].rearrange("m (t r u) -> m t r u", t=2, u=2),
+                turned[:].rearrange("m (t u r) -> m t r u", t=2, u=2),
+                on_vector,
+            )
+
+        pair_sums = {}
         lengths = {}
         one_plus_sq = {}
         denom_sq = {}
         seeds = {}
+        seeds_sq = {}
+        roughs = {}
+        x_y_sqs = {}
         factors = {}
         result = {}
 
-        def square_bank(group, oh):
-            if oh == 0:
-                squares_tile = work.tile([P, O_HIGH * BLOCKS_PER_HIGH, GROUP_TILES, P], F32)
-                squares[group] = squares_tile
-            first_row = (group % GROUPS_PER_CHUNK) * GROUP_TILES * P
-            acc = psum_norm.tile([P, BLOCKS_PER_HIGH, GROUP_TILES * P], F32)
-            for block in range(BLOCKS_PER_HIGH):
-                first_col = (group // GROUPS_PER_CHUNK) * CHUNK + (oh * BLOCKS_PER_HIGH + block) * P
+        norm_banks = {}
+        out_banks = {}
+
+        def norm_product(group, k):
+            first_row = (group % GROUPS_PER_CHUNK) * GROUP_ROWS
+            acc = psum_banks.tile([P, O_NORM, GROUP_ROWS], F32, tag="bank")
+            for ob in range(O_NORM):
+                first_col = (group // GROUPS_PER_CHUNK) * CHUNK + (k * O_NORM + ob) * J_CHUNK
                 nc.tensor.matmul_mx(
-                    out=acc[:, block, :],
+                    out=acc[:, ob, :],
                     lhsT=w_codes[:, first_col : first_col + P].bitcast(FP8X4),
                     lhsT_scale=w_scales[:, first_col : first_col + P],
-                    rhs=p_codes[:, first_row : first_row + GROUP_TILES * P].bitcast(FP8X4),
-                    rhs_scale=p_scales[:, first_row : first_row + GROUP_TILES * P],
+                    rhs=p_codes[:, first_row : first_row + GROUP_ROWS].bitcast(FP8X4),
+                    rhs_scale=p_scales[:, first_row : first_row + GROUP_ROWS],
                     start=True,
                     stop=True,
                 )
-            nc.scalar.activation(
-                out=squares[group][:, oh * BLOCKS_PER_HIGH : (oh + 1) * BLOCKS_PER_HIGH, :, :].rearrange(
-                    "q b t r -> q b (t r)"
-                ),
-                in_=acc[:],
-                func=ACT.Square,
-                scale=COUPLING,
+            norm_banks[(group, k)] = acc
+
+        def square_bank(group, k):
+            if k == 0:
+                pair_tile = pair_pool.tile([P, GROUP_BANKS, GROUP_ROWS], F32)
+                pair_sums[group] = pair_tile
+            acc = norm_banks[(group, k)]
+            squares = squares_pool.tile([P, O_NORM, GROUP_ROWS], F32)
+            nc.scalar.activation(out=squares[:], in_=acc[:], func=ACT.Square, scale=COUPLING)
+            nc.gpsimd.tensor_tensor(
+                out=pair_sums[group][:, k, :], in0=squares[:, 0, :], in1=squares[:, 1, :], op=ALU.add
             )
 
-        def sum_squares(group):
-            sums = psum_sums.tile([P, GROUP_TILES, BLOCKS_PER_HIGH, P], F32)
-            for tile_in_group in range(GROUP_TILES):
-                for block in range(BLOCKS_PER_HIGH):
-                    for oh in range(O_HIGH):
-                        nc.tensor.matmul(
-                            out=sums[:, tile_in_group, block, :],
-                            lhsT=squares[group][:, oh * BLOCKS_PER_HIGH + block, tile_in_group, :],
-                            rhs=ident[:],
-                            is_transpose=True,
-                            start=(oh == 0),
-                            stop=(oh == O_HIGH - 1),
-                        )
-            partial_sums[group] = sums
-
-        def factor_lengths(group):
-            q = work.tile([P, GROUP_J], F32)
-            nc.vector.tensor_reduce(
-                out=q[:],
-                in_=partial_sums[group][:].rearrange("r t b (j l) -> r (t b j) l", l=O_LOW),
-                axis=mybir.AxisListType.X,
-                op=ALU.add,
-            )
-            lengths[group] = q
+        def sum_squares(group, tile_in_group):
+            if tile_in_group == 0:
+                q = psum_sums.tile([P, GROUP_TILES, J_CHUNK], F32)
+                lengths[group] = q
+            for k in range(GROUP_BANKS):
+                nc.tensor.matmul(
+                    out=lengths[group][:, tile_in_group, :],
+                    lhsT=pair_sums[group][:, k, tile_in_group * P : (tile_in_group + 1) * P],
+                    rhs=ident[:],
+                    is_transpose=True,
+                    start=(k == 0),
+                    stop=(k == GROUP_BANKS - 1),
+                )
 
         def factor_one_plus_q(group):
-            one_plus_q_sq = work.tile([P, GROUP_J], F32)
+            one_plus_q_sq = work.tile([P, GROUP_TILES, J_CHUNK], F32)
             nc.scalar.activation(
-                out=one_plus_q_sq[:],
-                in_=lengths[group][:],
-                func=ACT.Square,
-                scale=SHRINK,
-                bias=shrink_col[:],
+                out=one_plus_q_sq[:], in_=lengths[group][:], func=ACT.Square, scale=SHRINK, bias=shrink_col[:]
             )
             one_plus_sq[group] = one_plus_q_sq
 
         def factor_denominator(group):
-            x = work.tile([P, GROUP_J], F32)
+            x = work.tile([P, GROUP_TILES, J_CHUNK], F32)
             nc.vector.scalar_tensor_tensor(
                 out=x[:],
                 in0=lengths[group][:],
@@ -254,40 +263,53 @@ def tile_capsulenetwork_pb_kernel(tc, p, Wr, out):
             denom_sq[group] = x
 
         def factor_seed(group):
-            y = work.tile([P, GROUP_J], F32)
+            y = work.tile([P, GROUP_TILES, J_CHUNK], F32)
             nc.scalar.activation(out=y[:], in_=denom_sq[group][:], func=ACT.Abs_reciprocal_sqrt)
-            y_sq = work.tile([P, GROUP_J], F32)
-            nc.scalar.activation(out=y_sq[:], in_=y[:], func=ACT.Square)
-            seeds[group] = (y, y_sq)
+            seeds[group] = y
 
-        def factor_newton(group):
-            y, y_sq = seeds[group]
-            x_y_sq = work.tile([P, GROUP_J], F32)
-            nc.vector.tensor_tensor(out=x_y_sq[:], in0=denom_sq[group][:], in1=y_sq[:], op=ALU.mult)
-            rough = work.tile([P, GROUP_J], F32)
+        def factor_seed_sq(group):
+            y_sq = work.tile([P, GROUP_TILES, J_CHUNK], F32)
+            nc.scalar.activation(out=y_sq[:], in_=seeds[group][:], func=ACT.Square)
+            seeds_sq[group] = y_sq
+
+        def factor_rough(group):
+            rough = work.tile([P, GROUP_TILES, J_CHUNK], F32)
             nc.vector.scalar_tensor_tensor(
                 out=rough[:],
                 in0=lengths[group][:],
                 scalar=-0.5 * SHRINK * COUPLING,
-                in1=y[:],
+                in1=seeds[group][:],
                 op0=ALU.mult,
                 op1=ALU.mult,
             )
-            factor = work.tile([P, GROUP_J], F32)
+            roughs[group] = rough
+
+        def factor_x_y_sq(group):
+            x_y_sq = work.tile([P, GROUP_TILES, J_CHUNK], F32)
+            nc.vector.tensor_tensor(out=x_y_sq[:], in0=denom_sq[group][:], in1=seeds_sq[group][:], op=ALU.mult)
+            x_y_sqs[group] = x_y_sq
+
+        def factor_newton(group):
+            factor = work.tile([P, GROUP_TILES, J_CHUNK], F32)
             nc.vector.scalar_tensor_tensor(
-                out=factor[:], in0=x_y_sq[:], scalar=3.0, in1=rough[:], op0=ALU.subtract, op1=ALU.mult
+                out=factor[:],
+                in0=x_y_sqs[group][:],
+                scalar=3.0,
+                in1=roughs[group][:],
+                op0=ALU.subtract,
+                op1=ALU.mult,
             )
             factors[group] = factor
 
-        def output_bank(group, k):
-            tile_in_group = k // 2
-            half = k % 2
+        def out_product(group, k):
+            tile_in_group = k // 4
+            quarter = k % 4
             t = GROUP_TILES * (group % GROUPS_PER_CHUNK) + tile_in_group
             c = group // GROUPS_PER_CHUNK
-            first_col = c * CHUNK + half * BANK
-            acc = psum_out.tile([P, HIGH_PER_BANK, J_CHUNK, O_LOW], F32)
+            first_col = c * CHUNK + quarter * BANK
+            acc = psum_banks.tile([P, O_OUT, J_CHUNK], F32, tag="bank")
             nc.tensor.matmul_mx(
-                out=acc[:].rearrange("r h j l -> r (h j l)"),
+                out=acc[:].rearrange("r o j -> r (o j)"),
                 lhsT=p_codes[:, t * P : (t + 1) * P].bitcast(FP8X4),
                 lhsT_scale=p_scales[:, t * P : (t + 1) * P],
                 rhs=w_codes[:, first_col : first_col + BANK].bitcast(FP8X4),
@@ -295,47 +317,108 @@ def tile_capsulenetwork_pb_kernel(tc, p, Wr, out):
                 start=True,
                 stop=True,
             )
-            if half == 0:
-                result_tile = results.tile([P, J_CHUNK, O_HIGH, O_LOW], F32)
+            out_banks[(group, k)] = acc
+
+        def scale_bank(group, k):
+            tile_in_group = k // 4
+            quarter = k % 4
+            t = GROUP_TILES * (group % GROUPS_PER_CHUNK) + tile_in_group
+            c = group // GROUPS_PER_CHUNK
+            acc = out_banks[(group, k)]
+            if quarter == 0:
+                result_tile = results.tile([P, J_CHUNK, O], F32)
                 result[group] = result_tile
             nc.vector.tensor_tensor(
-                out=result[group][:, :, half * HIGH_PER_BANK : (half + 1) * HIGH_PER_BANK, :],
-                in0=acc[:].rearrange("r h j l -> r j h l"),
-                in1=factors[group][:, tile_in_group * J_CHUNK : (tile_in_group + 1) * J_CHUNK]
-                .unsqueeze(2)
-                .unsqueeze(3)
-                .to_broadcast([P, J_CHUNK, HIGH_PER_BANK, O_LOW]),
+                out=result[group][:, :, quarter * O_OUT : (quarter + 1) * O_OUT],
+                in0=acc[:].rearrange("r o j -> r j o"),
+                in1=factors[group][:, tile_in_group, :].unsqueeze(2).to_broadcast([P, J_CHUNK, O_OUT]),
                 op=ALU.mult,
             )
-            if half == 1:
+            if quarter == 3:
                 nc.sync.dma_start(
                     out=out_rows[:, t, c * CHUNK : (c + 1) * CHUNK],
-                    in_=result[group][:].rearrange("r j h l -> r (j h l)"),
+                    in_=result[group][:].rearrange("r j o -> r (j o)"),
                 )
 
-        for i in range(N_GROUPS + LAG_OUTPUT):
-            prepare = 1 <= i < N_CHUNKS
-            if prepare:
-                sort_w(i)
-            for k in range(GROUP_BANKS):
-                if i < N_GROUPS:
-                    square_bank(i, k)
-                if k == 0 and i >= LAG_OUTPUT:
-                    factor_newton(i - LAG_OUTPUT)
-                if 0 <= i - LAG_FACTOR < N_GROUPS:
-                    if k == 0:
-                        factor_lengths(i - LAG_FACTOR)
-                    if k == 1:
-                        factor_one_plus_q(i - LAG_FACTOR)
-                    if k == 2:
-                        factor_denominator(i - LAG_FACTOR)
-                    if k == 3:
-                        factor_seed(i - LAG_FACTOR)
-                if i >= LAG_OUTPUT:
-                    output_bank(i - LAG_OUTPUT, k)
-                if prepare:
-                    turn_w(i, k, on_vector=(i < LAG_OUTPUT))
-            if prepare:
-                quantise_w(i)
-            if 0 <= i - LAG_SUMS < N_GROUPS:
-                sum_squares(i - LAG_SUMS)
+        AHEAD_NORM = 2
+        AHEAD_OUT = 2
+        LAG_SUMS = 2
+        LAG_Q = 5
+        LAG_OUT = 10
+        LAST = GROUP_BANKS - 1
+        N_STEPS = N_GROUPS * GROUP_BANKS
+        PAIRS = B_TILES // 2
+        N_TURNS = O // O_TURN
+        P_TURN = 2
+        W1_SORT = 4
+        W1_TURN = 10
+        W1_EVERY = 3
+        ctx.enter_context(tc.manual_schedule())
+        sort_p(0)
+        turn_p(0)
+        group_p(0, on_vector=False)
+        for piece in range(PIECES):
+            sort_w(0, piece)
+            if piece == 1:
+                quantise_p(0)
+        HEAD = 4
+        for bank in range(N_TURNS + HEAD):
+            if bank < N_TURNS:
+                turn_w(0, bank)
+            done = bank - HEAD
+            if done >= 0:
+                group_w(0, done, on_vector=(done not in (0, 2, 3, 5, 6)))
+                if done % 2 == 1:
+                    quantise_w(0, done // 2)
+                    if done // 2 + 1 < PAIRS:
+                        sort_p(done // 2 + 1)
+        for step in range(-AHEAD_NORM, N_STEPS + LAST + LAG_OUT + 1):
+            ahead = step + AHEAD_NORM
+            if ahead < N_STEPS:
+                norm_product(ahead // GROUP_BANKS, ahead % GROUP_BANKS)
+            if 0 <= step < N_STEPS:
+                square_bank(step // GROUP_BANKS, step % GROUP_BANKS)
+            if P_TURN <= step < P_TURN + PAIRS - 1:
+                turn_p(step - P_TURN + 1)
+            if P_TURN + 1 <= step < P_TURN + PAIRS:
+                group_p(step - P_TURN, on_vector=False)
+            if P_TURN + 2 <= step < P_TURN + 1 + PAIRS:
+                quantise_p(step - P_TURN - 1)
+            if W1_SORT <= step < W1_SORT + PIECES:
+                sort_w(1, step - W1_SORT)
+            turns, rest = divmod(step - W1_TURN, W1_EVERY)
+            if 0 <= turns < N_TURNS // 2 and rest == 0:
+                turn_w(1, 2 * turns)
+                turn_w(1, 2 * turns + 1)
+            turns, rest = divmod(step - W1_TURN - 1, W1_EVERY)
+            if 0 <= turns < N_TURNS // 2 and rest == 0:
+                group_w(1, 2 * turns, on_vector=False)
+                group_w(1, 2 * turns + 1, on_vector=True)
+            turns, rest = divmod(step - W1_TURN - 3, W1_EVERY)
+            if 0 <= turns < N_TURNS // 2 and rest == 0:
+                quantise_w(1, turns)
+            group, offset = divmod(step - LAST, GROUP_BANKS)
+            for back in range(3):
+                g, off = group - back, offset + back * GROUP_BANKS
+                if 0 <= g < N_GROUPS:
+                    if LAG_SUMS <= off < LAG_SUMS + GROUP_TILES:
+                        sum_squares(g, off - LAG_SUMS)
+                    if off == LAG_Q:
+                        factor_one_plus_q(g)
+                    if off == LAG_Q + 1:
+                        factor_denominator(g)
+                    if off == LAG_Q + 2:
+                        factor_seed(g)
+                    if off == LAG_Q + 3:
+                        factor_seed_sq(g)
+                        factor_rough(g)
+                    if off == LAG_Q + 4:
+                        factor_x_y_sq(g)
+                    if off == LAG_Q + 5:
+                        factor_newton(g)
+            ahead = step - LAST - LAG_OUT + AHEAD_OUT
+            if 0 <= ahead < N_STEPS:
+                out_product(ahead // GROUP_BANKS, ahead % GROUP_BANKS)
+            done = step - LAST - LAG_OUT
+            if 0 <= done < N_STEPS:
+                scale_bank(done // GROUP_BANKS, done % GROUP_BANKS)

@@ -52,8 +52,8 @@ def tile_capsulenetwork_pb_kernel(tc, p, Wr, out):
         keep = ctx.enter_context(tc.tile_pool(name="keep", bufs=1))
         stage = ctx.enter_context(tc.tile_pool(name="stage", bufs=2))
         quarters = ctx.enter_context(tc.tile_pool(name="quarters", bufs=4))
-        squares_pool = ctx.enter_context(tc.tile_pool(name="squares_pool", bufs=6))
-        pair_pool = ctx.enter_context(tc.tile_pool(name="pair_pool", bufs=3))
+        squares_pool = ctx.enter_context(tc.tile_pool(name="squares_pool", bufs=16))
+        pair_pool = ctx.enter_context(tc.tile_pool(name="pair_pool", bufs=2))
         work = ctx.enter_context(tc.tile_pool(name="work", bufs=3))
         results = ctx.enter_context(tc.tile_pool(name="results", bufs=4))
         psum_banks = ctx.enter_context(tc.psum_pool(name="psum_banks", bufs=7))
@@ -189,6 +189,8 @@ def tile_capsulenetwork_pb_kernel(tc, p, Wr, out):
             )
 
         pair_sums = {}
+        summands = {}
+        FIRST_ADDED = 1
         lengths = {}
         one_plus_sq = {}
         denom_sq = {}
@@ -219,28 +221,32 @@ def tile_capsulenetwork_pb_kernel(tc, p, Wr, out):
             norm_banks[(group, k)] = acc
 
         def square_bank(group, k):
-            if k == 0:
-                pair_tile = pair_pool.tile([P, GROUP_BANKS, GROUP_ROWS], F32)
-                pair_sums[group] = pair_tile
             acc = norm_banks[(group, k)]
             squares = squares_pool.tile([P, O_NORM, GROUP_ROWS], F32)
             nc.scalar.activation(out=squares[:], in_=acc[:], func=ACT.Square, scale=COUPLING)
-            nc.gpsimd.tensor_tensor(
-                out=pair_sums[group][:, k, :], in0=squares[:, 0, :], in1=squares[:, 1, :], op=ALU.add
-            )
+            if group < FIRST_ADDED:
+                summands.setdefault(group, []).extend([squares[:, ob, :] for ob in range(O_NORM)])
+            else:
+                if k == 0:
+                    pair_tile = pair_pool.tile([P, GROUP_BANKS, GROUP_ROWS], F32)
+                    pair_sums[group] = pair_tile
+                pair_sum = pair_sums[group][:, k, :]
+                nc.gpsimd.tensor_tensor(out=pair_sum, in0=squares[:, 0, :], in1=squares[:, 1, :], op=ALU.add)
+                summands.setdefault(group, []).append(pair_sum)
 
         def sum_squares(group, tile_in_group):
             if tile_in_group == 0:
                 q = psum_sums.tile([P, GROUP_TILES, J_CHUNK], F32)
                 lengths[group] = q
-            for k in range(GROUP_BANKS):
+            rows = slice(tile_in_group * P, (tile_in_group + 1) * P)
+            for k, summand in enumerate(summands[group]):
                 nc.tensor.matmul(
                     out=lengths[group][:, tile_in_group, :],
-                    lhsT=pair_sums[group][:, k, tile_in_group * P : (tile_in_group + 1) * P],
+                    lhsT=summand[:, rows],
                     rhs=ident[:],
                     is_transpose=True,
                     start=(k == 0),
-                    stop=(k == GROUP_BANKS - 1),
+                    stop=(k == len(summands[group]) - 1),
                 )
 
         def factor_one_plus_q(group):

@@ -236,7 +236,7 @@ def tile_capsulenetwork_pb_kernel(tc, p, Wr, out):
 
         def sum_squares(group, tile_in_group):
             if tile_in_group == 0:
-                q = psum_sums.tile([P, GROUP_TILES, J_CHUNK], F32)
+                q = psum_sums.tile([P, GROUP_TILES, J_CHUNK], F32, tag="sums")
                 lengths[group] = q
             rows = slice(tile_in_group * P, (tile_in_group + 1) * P)
             for k, summand in enumerate(summands[group]):
@@ -363,8 +363,23 @@ def tile_capsulenetwork_pb_kernel(tc, p, Wr, out):
         sort_p(0)
         turn_p(0)
         group_p(0, on_vector=False)
+        warm_up = psum_sums.tile([P, BANK], F32, tag="sums")
+
+        def keep_warm(piece):
+            for n in range(piece * N_PIECE, piece * N_PIECE + 2 * WARM_MATMULS, 2):
+                nc.tensor.matmul(
+                    out=warm_up[:],
+                    lhsT=p_raw[:, 0, :P],
+                    rhs=w_raws[0][:, n : n + 2, :].rearrange("q n x -> q (n x)"),
+                    start=True,
+                    stop=True,
+                )
+
+        WARM_MATMULS = 3
         for piece in range(PIECES):
             sort_w(0, piece)
+            if piece in (1, 2):
+                keep_warm(piece)
             if piece == 1:
                 quantise_p(0)
         HEAD = 4

@@ -33,6 +33,7 @@ GROUP_TILES = 2
 GROUP_ROWS = GROUP_TILES * P
 O_NORM = BANK // GROUP_ROWS
 GROUP_BANKS = 8
+TILE_BANKS = GROUP_BANKS // GROUP_TILES
 GROUP_Q = GROUP_TILES * J_CHUNK
 GROUPS_PER_CHUNK = B_TILES // GROUP_TILES
 N_GROUPS = N_CHUNKS * GROUPS_PER_CHUNK
@@ -56,6 +57,7 @@ def tile_capsulenetwork_pb_kernel(tc, p, Wr, out):
         pair_pool = ctx.enter_context(tc.tile_pool(name="pair_pool", bufs=2))
         work = ctx.enter_context(tc.tile_pool(name="work", bufs=3))
         results = ctx.enter_context(tc.tile_pool(name="results", bufs=4))
+        copied_pool = ctx.enter_context(tc.tile_pool(name="copied_pool", bufs=2))
         psum_banks = ctx.enter_context(tc.psum_pool(name="psum_banks", bufs=7))
         psum_sums = ctx.enter_context(tc.psum_pool(name="psum_sums", bufs=1))
 
@@ -190,7 +192,6 @@ def tile_capsulenetwork_pb_kernel(tc, p, Wr, out):
 
         pair_sums = {}
         summands = {}
-        FIRST_ADDED = 1
         lengths = {}
         one_plus_sq = {}
         denom_sq = {}
@@ -224,10 +225,10 @@ def tile_capsulenetwork_pb_kernel(tc, p, Wr, out):
             acc = norm_banks[(group, k)]
             squares = squares_pool.tile([P, O_NORM, GROUP_ROWS], F32)
             nc.scalar.activation(out=squares[:], in_=acc[:], func=ACT.Square, scale=COUPLING)
-            if group < FIRST_ADDED:
+            if k in (UNADDED_FIRST if group == 0 else UNADDED_LAST if group == N_GROUPS - 1 else UNADDED):
                 summands.setdefault(group, []).extend([squares[:, ob, :] for ob in range(O_NORM)])
             else:
-                if k == 0:
+                if group not in pair_sums:
                     pair_tile = pair_pool.tile([P, GROUP_BANKS, GROUP_ROWS], F32)
                     pair_sums[group] = pair_tile
                 pair_sum = pair_sums[group][:, k, :]
@@ -325,39 +326,65 @@ def tile_capsulenetwork_pb_kernel(tc, p, Wr, out):
             )
             out_banks[(group, k)] = acc
 
-        def scale_bank(group, k):
-            tile_in_group = k // 4
-            quarter = k % 4
+        copied_banks = {}
+        unscaled = {}
+
+        def copy_bank(group, k):
+            copied = copied_pool.tile([P, J_CHUNK, O_OUT], F32)
+            nc.scalar.copy(out=copied[:], in_=out_banks[(group, k)][:].rearrange("r o j -> r j o"))
+            copied_banks[(group, k)] = copied
+
+        def scale_bank(group, k, half=None):
+            tile_in_group, quarter = divmod(k, TILE_BANKS)
             t = GROUP_TILES * (group % GROUPS_PER_CHUNK) + tile_in_group
             c = group // GROUPS_PER_CHUNK
-            acc = out_banks[(group, k)]
-            if quarter == 0:
+            if (group, tile_in_group) not in result:
                 result_tile = results.tile([P, J_CHUNK, O], F32)
-                result[group] = result_tile
-            nc.vector.tensor_tensor(
-                out=result[group][:, :, quarter * O_OUT : (quarter + 1) * O_OUT],
-                in0=acc[:].rearrange("r o j -> r j o"),
-                in1=factors[group][:, tile_in_group, :].unsqueeze(2).to_broadcast([P, J_CHUNK, O_OUT]),
+                result[(group, tile_in_group)] = result_tile
+            n_j = J_CHUNK if half is None else J_CHUNK // 2
+            first_j = 0 if half is None else half * n_j
+            j = slice(first_j, first_j + n_j)
+            aside = (group, k) in copied_banks
+            bank = copied_banks[(group, k)][:] if aside else out_banks[(group, k)][:].rearrange("r o j -> r j o")
+            engine = nc.gpsimd if aside else nc.vector
+            engine.tensor_tensor(
+                out=result[(group, tile_in_group)][:, j, quarter * O_OUT : (quarter + 1) * O_OUT],
+                in0=bank[:, j, :],
+                in1=factors[group][:, tile_in_group, j].unsqueeze(2).to_broadcast([P, n_j, O_OUT]),
                 op=ALU.mult,
             )
-            if quarter == 3:
+            part = (group, tile_in_group, half)
+            unscaled[part] = unscaled.get(part, TILE_BANKS) - 1
+            if unscaled[part] == 0:
+                first_col = c * CHUNK + first_j * O
                 nc.sync.dma_start(
-                    out=out_rows[:, t, c * CHUNK : (c + 1) * CHUNK],
-                    in_=result[group][:].rearrange("r j o -> r (j o)"),
+                    out=out_rows[:, t, first_col : first_col + n_j * O],
+                    in_=result[(group, tile_in_group)][:, j, :].rearrange("r j o -> r (j o)"),
                 )
 
         AHEAD_NORM = 2
         AHEAD_OUT = 2
-        LAG_SUMS = 2
-        LAG_Q = 5
-        LAG_OUT = 10
+        LAGS = (1, 1, 3, 5, 6, 8, 8, 9, 9)
+        LAGS_FIRST = (1, 4, 5, 6, 7, 7, 8, 9, 10)
+        LAGS_LAST = (2, 4, 5, 6, 8, 9, 8, 10, 11)
+        UNADDED_FIRST = (2, 3, 4, 5, 6, 7)
+        UNADDED = (7,)
+        UNADDED_LAST = (6, 7)
+        P_MERGE = 0
+        P_SORT = 1
+        W1_QUANT = 3
+        W1_ON_V = (1, 3, 5, 7)
+        W1_SORT_EVERY = 1
+        HEAD_V = (1, 3, 6)
+        SUMS_END = 0
+        OUT_EARLY = 0
         LAST = GROUP_BANKS - 1
         N_STEPS = N_GROUPS * GROUP_BANKS
         PAIRS = B_TILES // 2
         N_TURNS = O // O_TURN
         P_TURN = 2
-        W1_SORT = 4
-        W1_TURN = 10
+        W1_SORT = 1
+        W1_TURN = 6
         W1_EVERY = 3
         ctx.enter_context(tc.manual_schedule())
         sort_p(0)
@@ -382,64 +409,96 @@ def tile_capsulenetwork_pb_kernel(tc, p, Wr, out):
                 keep_warm(piece)
             if piece == 1:
                 quantise_p(0)
+        ASIDE_LIST = ((6, 0), (6, 1))
+        ASIDE = ASIDE_LIST
+        out_steps = {}
+        out_step = 0
+        for group in range(N_GROUPS):
+            lags = LAGS_FIRST if group == 0 else LAGS_LAST if group == N_GROUPS - 1 else LAGS
+            out_step = max(out_step, group * GROUP_BANKS + LAST + lags[-1])
+            for k in range(GROUP_BANKS):
+                out_steps.setdefault(out_step, []).append((group, k))
+                if (group, k) not in ASIDE:
+                    out_step += 1
+        last_scaling = out_step - 1
         HEAD = 4
+        if P_SORT:
+            for pair in range(1, PAIRS):
+                sort_p(pair)
         for bank in range(N_TURNS + HEAD):
             if bank < N_TURNS:
                 turn_w(0, bank)
             done = bank - HEAD
             if done >= 0:
-                group_w(0, done, on_vector=(done not in (0, 2, 3, 5, 6)))
+                group_w(0, done, on_vector=(done in HEAD_V))
                 if done % 2 == 1:
                     quantise_w(0, done // 2)
-                    if done // 2 + 1 < PAIRS:
+                    if done // 2 + 1 < PAIRS and not P_SORT:
                         sort_p(done // 2 + 1)
-        for step in range(-AHEAD_NORM, N_STEPS + LAST + LAG_OUT + 1):
+        for step in range(-AHEAD_NORM, N_STEPS + LAST + 12):
+            if OUT_EARLY:
+                for group, k in out_steps.get(step + AHEAD_OUT, ()):
+                    out_product(group, k)
+                    if (group, k) in ASIDE:
+                        copy_bank(group, k)
             ahead = step + AHEAD_NORM
             if ahead < N_STEPS:
                 norm_product(ahead // GROUP_BANKS, ahead % GROUP_BANKS)
             if 0 <= step < N_STEPS:
                 square_bank(step // GROUP_BANKS, step % GROUP_BANKS)
-            if P_TURN <= step < P_TURN + PAIRS - 1:
-                turn_p(step - P_TURN + 1)
-            if P_TURN + 1 <= step < P_TURN + PAIRS:
-                group_p(step - P_TURN, on_vector=False)
-            if P_TURN + 2 <= step < P_TURN + 1 + PAIRS:
-                quantise_p(step - P_TURN - 1)
-            if W1_SORT <= step < W1_SORT + PIECES:
-                sort_w(1, step - W1_SORT)
-            turns, rest = divmod(step - W1_TURN, W1_EVERY)
-            if 0 <= turns < N_TURNS // 2 and rest == 0:
-                turn_w(1, 2 * turns)
-                turn_w(1, 2 * turns + 1)
-            turns, rest = divmod(step - W1_TURN - 1, W1_EVERY)
-            if 0 <= turns < N_TURNS // 2 and rest == 0:
-                group_w(1, 2 * turns, on_vector=False)
-                group_w(1, 2 * turns + 1, on_vector=True)
-            turns, rest = divmod(step - W1_TURN - 3, W1_EVERY)
-            if 0 <= turns < N_TURNS // 2 and rest == 0:
-                quantise_w(1, turns)
+            for pair in range(1, PAIRS):
+                turn_step = P_TURN + (0 if P_MERGE else pair - 1)
+                if step == turn_step:
+                    turn_p(pair)
+            for pair in range(1, PAIRS):
+                if step == P_TURN + pair:
+                    group_p(pair, on_vector=False)
+                if step == P_TURN + pair + 1:
+                    quantise_p(pair)
+            for piece in range(PIECES):
+                if step == W1_SORT + piece * W1_SORT_EVERY:
+                    sort_w(1, piece)
+            for turns in range(N_TURNS // 2):
+                if step == W1_TURN + turns * W1_EVERY:
+                    turn_w(1, 2 * turns)
+                    turn_w(1, 2 * turns + 1)
+                if step == W1_TURN + turns * W1_EVERY + 1:
+                    group_w(1, 2 * turns, 2 * turns in W1_ON_V)
+                    group_w(1, 2 * turns + 1, 2 * turns + 1 in W1_ON_V)
+                if step == W1_TURN + turns * W1_EVERY + W1_QUANT:
+                    quantise_w(1, turns)
             group, offset = divmod(step - LAST, GROUP_BANKS)
-            for back in range(3):
-                g, off = group - back, offset + back * GROUP_BANKS
-                if 0 <= g < N_GROUPS:
-                    if LAG_SUMS <= off < LAG_SUMS + GROUP_TILES:
-                        sum_squares(g, off - LAG_SUMS)
-                    if off == LAG_Q:
-                        factor_one_plus_q(g)
-                    if off == LAG_Q + 1:
-                        factor_denominator(g)
-                    if off == LAG_Q + 2:
-                        factor_seed(g)
-                    if off == LAG_Q + 3:
-                        factor_seed_sq(g)
-                        factor_rough(g)
-                    if off == LAG_Q + 4:
-                        factor_x_y_sq(g)
-                    if off == LAG_Q + 5:
-                        factor_newton(g)
-            ahead = step - LAST - LAG_OUT + AHEAD_OUT
-            if 0 <= ahead < N_STEPS:
-                out_product(ahead // GROUP_BANKS, ahead % GROUP_BANKS)
-            done = step - LAST - LAG_OUT
-            if 0 <= done < N_STEPS:
-                scale_bank(done // GROUP_BANKS, done % GROUP_BANKS)
+            for late in (0, 1):
+                for back in range(3):
+                    g, off = group - back, offset + back * GROUP_BANKS
+                    if 0 <= g < N_GROUPS:
+                        lags = LAGS_FIRST if g == 0 else LAGS_LAST if g == N_GROUPS - 1 else LAGS
+                        actions = (
+                            factor_one_plus_q,
+                            factor_denominator,
+                            factor_seed,
+                            factor_seed_sq,
+                            factor_rough,
+                            factor_x_y_sq,
+                            factor_newton,
+                        )
+                        if late == SUMS_END:
+                            for tile_in_group in range(GROUP_TILES):
+                                if off == lags[tile_in_group]:
+                                    sum_squares(g, tile_in_group)
+                        if late == 0:
+                            for lag, action in zip(lags[GROUP_TILES:], actions):
+                                if off == lag:
+                                    action(g)
+            if not OUT_EARLY:
+                for group, k in out_steps.get(step + AHEAD_OUT, ()):
+                    out_product(group, k)
+                    if (group, k) in ASIDE:
+                        copy_bank(group, k)
+            for group, k in out_steps.get(step, ()):
+                if group < N_GROUPS - 1 or k < GROUP_BANKS - TILE_BANKS:
+                    scale_bank(group, k)
+            if step == last_scaling:
+                for half in range(2):
+                    for k in range(GROUP_BANKS - TILE_BANKS, GROUP_BANKS):
+                        scale_bank(N_GROUPS - 1, k, half)

@@ -23,6 +23,7 @@ B_TILES = B // P
 G = N_CAPS // 2
 BANK = 512
 J_CHUNK = 128
+J_PAIRS = J_CHUNK // 2
 CHUNK = J_CHUNK * O
 N_CHUNKS = J // J_CHUNK
 O_TURN = 2
@@ -69,22 +70,29 @@ def tile_capsulenetwork_pb_kernel(tc, p, Wr, out):
                 out=p_raw[:, tiles, :], in_=p.rearrange("(r t) n i -> r t (n i)", t=B_TILES)[:, tiles, :]
             )
 
-        load_p(0)
         w_raws = []
         PIECES = 4
-        N_PIECE = N_CAPS // PIECES
-        for c in range(N_CHUNKS):
-            w_raw = stage.tile([P, N_CAPS, O * I], BF16)
+        G_PIECE = G // PIECES
+
+        def load_w(c):
+            w_raw = stage.tile([P, G, 2 * O * I], BF16)
             w_raws.append(w_raw)
+            by_half = Wr[:, c * J_CHUNK : (c + 1) * J_CHUNK, :, :].rearrange(
+                "(g u) (jp jl) o i -> u jp g (jl o i)", u=2, jl=2
+            )
             for piece in range(PIECES):
-                caps = slice(piece * N_PIECE, (piece + 1) * N_PIECE)
-                nc.sync.dma_start(
-                    out=w_raw[:, caps, :],
-                    in_=Wr[caps, c * J_CHUNK : (c + 1) * J_CHUNK, :, :].rearrange("n j o i -> j n (o i)"),
-                )
-            if c == 0:
-                for pair in range(1, B_TILES // 2):
-                    load_p(pair)
+                pairs = slice(piece * G_PIECE, (piece + 1) * G_PIECE)
+                for u in range(2):
+                    nc.sync.dma_start(out=w_raw[u:P:2, pairs, :], in_=by_half[u, :, pairs, :])
+
+        P_AFTER = 0
+        load_p(0)
+        load_w(0)
+        for pair in range(1, B_TILES // 2 - P_AFTER):
+            load_p(pair)
+        load_w(1)
+        for pair in range(B_TILES // 2 - P_AFTER, B_TILES // 2):
+            load_p(pair)
 
         shrink_col = keep.tile([P, 1], F32)
         nc.vector.memset(shrink_col[:], SHRINK)
@@ -110,23 +118,22 @@ def tile_capsulenetwork_pb_kernel(tc, p, Wr, out):
 
         def sort_w(c, piece):
             if piece == 0:
-                sorted_tile = stage.tile([P, O, 2, G, I], BF16)
+                sorted_tile = stage.tile([P, 2 * O, G, I], BF16)
                 w_sorted[c] = sorted_tile
-            by_half = w_raws[c][:].rearrange("q (g u) (o i) -> q u o g i", u=2, i=I)
-            pairs = slice(piece * N_PIECE // 2, (piece + 1) * N_PIECE // 2)
-            for u in range(2):
-                nc.vector.tensor_copy(out=w_sorted[c][:, :, u, pairs, :], in_=by_half[:, u, :, pairs, :])
+            pairs = slice(piece * G_PIECE, (piece + 1) * G_PIECE)
+            nc.vector.tensor_copy(
+                out=w_sorted[c][:, :, pairs, :],
+                in_=w_raws[c][:].rearrange("q g (lo i) -> q lo g i", i=I)[:, :, pairs, :],
+            )
 
         turned_banks = {}
 
         def turn_w(c, bank):
-            words = w_sorted[c][:].rearrange("q o u g i -> q (o u g i)").bitcast(F32)
+            words = w_sorted[c][:].rearrange("q lo g i -> q lo (g i)").bitcast(F32)
             turned = psum_banks.tile([P, BANK], F32, tag="bank")
-            for ou in range(O_TURN * 2):
-                first_word = (bank * O_TURN * 2 + ou) * P
-                nc.tensor.transpose(
-                    turned[:, ou * P : (ou + 1) * P], words[:, first_word : first_word + P], ident[:]
-                )
+            for block in range(O_TURN * 2):
+                o, jl = divmod(bank * O_TURN * 2 + block, 2)
+                nc.tensor.transpose(turned[:, block * P : (block + 1) * P], words[:, jl * O + o, :], ident[:])
             turned_banks[(c, bank)] = turned
 
         def group_w(c, bank, on_vector):
@@ -136,11 +143,7 @@ def tile_capsulenetwork_pb_kernel(tc, p, Wr, out):
                 quarter = quarters.tile([P, O_QUANT * J_CHUNK * 4], BF16, align_bytes=64)
                 w_quarters[(c, bank // 2)] = quarter
             copy_out_of_psum(
-                w_quarters[(c, bank // 2)][:].bitcast(F32)[:, half * BANK : (half + 1) * BANK].rearrange(
-                    "m (o j u) -> m o j u", o=O_TURN, u=2
-                ),
-                turned[:].rearrange("m (o u j) -> m o j u", o=O_TURN, u=2),
-                on_vector,
+                w_quarters[(c, bank // 2)][:].bitcast(F32)[:, half * BANK : (half + 1) * BANK], turned[:], on_vector
             )
 
         def quantise_w(c, quarter):
@@ -330,8 +333,8 @@ def tile_capsulenetwork_pb_kernel(tc, p, Wr, out):
         unscaled = {}
 
         def copy_bank(group, k):
-            copied = copied_pool.tile([P, J_CHUNK, O_OUT], F32)
-            nc.scalar.copy(out=copied[:], in_=out_banks[(group, k)][:].rearrange("r o j -> r j o"))
+            copied = copied_pool.tile([P, 2, J_PAIRS, O_OUT], F32)
+            nc.scalar.copy(out=copied[:], in_=out_banks[(group, k)][:].rearrange("r o (jl jp) -> r jl jp o", jl=2))
             copied_banks[(group, k)] = copied
 
         def scale_bank(group, k, half=None):
@@ -344,13 +347,19 @@ def tile_capsulenetwork_pb_kernel(tc, p, Wr, out):
             n_j = J_CHUNK if half is None else J_CHUNK // 2
             first_j = 0 if half is None else half * n_j
             j = slice(first_j, first_j + n_j)
+            jp = slice(first_j // 2, (first_j + n_j) // 2)
             aside = (group, k) in copied_banks
-            bank = copied_banks[(group, k)][:] if aside else out_banks[(group, k)][:].rearrange("r o j -> r j o")
+            bank = copied_banks[(group, k)][:] if aside else out_banks[(group, k)][:].rearrange("r o (jl jp) -> r jl jp o", jl=2)
             engine = nc.gpsimd if aside else nc.vector
             engine.tensor_tensor(
-                out=result[(group, tile_in_group)][:, j, quarter * O_OUT : (quarter + 1) * O_OUT],
-                in0=bank[:, j, :],
-                in1=factors[group][:, tile_in_group, j].unsqueeze(2).to_broadcast([P, n_j, O_OUT]),
+                out=result[(group, tile_in_group)][:].rearrange("r (jp jl) o -> r jl jp o", jl=2)[
+                    :, :, jp, quarter * O_OUT : (quarter + 1) * O_OUT
+                ],
+                in0=bank[:, :, jp, :],
+                in1=factors[group][:, tile_in_group, :]
+                .rearrange("r (jl jp) -> r jl jp", jl=2)[:, :, jp]
+                .unsqueeze(3)
+                .to_broadcast([P, 2, n_j // 2, O_OUT]),
                 op=ALU.mult,
             )
             part = (group, tile_in_group, half)
@@ -362,30 +371,30 @@ def tile_capsulenetwork_pb_kernel(tc, p, Wr, out):
                     in_=result[(group, tile_in_group)][:, j, :].rearrange("r j o -> r (j o)"),
                 )
 
-        AHEAD_NORM = 2
-        AHEAD_OUT = 2
-        LAGS = (1, 1, 3, 5, 6, 8, 8, 9, 9)
-        LAGS_FIRST = (1, 4, 5, 6, 7, 7, 8, 9, 10)
-        LAGS_LAST = (2, 4, 5, 6, 8, 9, 8, 10, 11)
+        AHEAD_NORM = 1
+        AHEAD_OUT = 1
+        LAGS = (2, 3, 4, 5, 6, 7, 8, 9, 9)
+        LAGS_FIRST = (2, 3, 5, 6, 7, 8, 7, 9, 10)
+        LAGS_LAST = (2, 2, 3, 4, 5, 6, 6, 7, 8)
         UNADDED_FIRST = (2, 3, 4, 5, 6, 7)
         UNADDED = (7,)
         UNADDED_LAST = (6, 7)
         P_MERGE = 0
         P_SORT = 1
-        W1_QUANT = 3
+        W1_QUANT = 2
         W1_ON_V = (1, 3, 5, 7)
         W1_SORT_EVERY = 1
-        HEAD_V = (1, 3, 6)
-        SUMS_END = 0
+        HEAD_V = (3, 5, 7)
+        SUMS_END = 1
         OUT_EARLY = 0
         LAST = GROUP_BANKS - 1
         N_STEPS = N_GROUPS * GROUP_BANKS
         PAIRS = B_TILES // 2
         N_TURNS = O // O_TURN
-        P_TURN = 2
+        P_TURN = 1
         W1_SORT = 1
-        W1_TURN = 6
-        W1_EVERY = 3
+        W1_TURN = 10
+        W1_EVERY = 2
         ctx.enter_context(tc.manual_schedule())
         sort_p(0)
         turn_p(0)
@@ -393,11 +402,11 @@ def tile_capsulenetwork_pb_kernel(tc, p, Wr, out):
         warm_up = psum_sums.tile([P, BANK], F32, tag="sums")
 
         def keep_warm(piece):
-            for n in range(piece * N_PIECE, piece * N_PIECE + 2 * WARM_MATMULS, 2):
+            for n in range(piece * G_PIECE, piece * G_PIECE + WARM_MATMULS):
                 nc.tensor.matmul(
                     out=warm_up[:],
                     lhsT=p_raw[:, 0, :P],
-                    rhs=w_raws[0][:, n : n + 2, :].rearrange("q n x -> q (n x)"),
+                    rhs=w_raws[0][:, n, :],
                     start=True,
                     stop=True,
                 )
@@ -421,7 +430,7 @@ def tile_capsulenetwork_pb_kernel(tc, p, Wr, out):
                 if (group, k) not in ASIDE:
                     out_step += 1
         last_scaling = out_step - 1
-        HEAD = 4
+        HEAD = 3
         if P_SORT:
             for pair in range(1, PAIRS):
                 sort_p(pair)

@@ -371,30 +371,30 @@ def tile_capsulenetwork_pb_kernel(tc, p, Wr, out):
                     in_=result[(group, tile_in_group)][:, j, :].rearrange("r j o -> r (j o)"),
                 )
 
-        AHEAD_NORM = 1
-        AHEAD_OUT = 1
-        LAGS = (2, 3, 4, 5, 6, 7, 8, 9, 9)
-        LAGS_FIRST = (2, 3, 5, 6, 7, 8, 7, 9, 10)
-        LAGS_LAST = (2, 2, 3, 4, 5, 6, 6, 7, 8)
-        UNADDED_FIRST = (2, 3, 4, 5, 6, 7)
+        AHEAD_NORM = 2
+        AHEAD_OUT = 2
+        LAGS = (1, 2, 4, 5, 6, 7, 8, 9, 9)
+        LAGS_FIRST = (1, 3, 5, 5, 7, 7, 8, 8, 10)
+        LAGS_LAST = (2, 3, 3, 4, 5, 6, 6, 7, 8)
+        UNADDED_FIRST = (0, 1, 2, 3, 4, 5, 6, 7)
         UNADDED = (7,)
-        UNADDED_LAST = (6, 7)
-        P_MERGE = 0
+        UNADDED_LAST = (7,)
+        P_MERGE = 1
         P_SORT = 1
-        W1_QUANT = 2
+        W1_QUANT = 3
         W1_ON_V = (1, 3, 5, 7)
         W1_SORT_EVERY = 1
-        HEAD_V = (3, 5, 7)
-        SUMS_END = 1
+        HEAD_V = (1, 4, 7)
+        SUMS_END = 0
         OUT_EARLY = 0
         LAST = GROUP_BANKS - 1
         N_STEPS = N_GROUPS * GROUP_BANKS
         PAIRS = B_TILES // 2
         N_TURNS = O // O_TURN
-        P_TURN = 1
+        P_TURN = 2
         W1_SORT = 1
-        W1_TURN = 10
-        W1_EVERY = 2
+        W1_TURN = 6
+        W1_EVERY = 3
         ctx.enter_context(tc.manual_schedule())
         sort_p(0)
         turn_p(0)
@@ -444,7 +444,7 @@ def tile_capsulenetwork_pb_kernel(tc, p, Wr, out):
                     quantise_w(0, done // 2)
                     if done // 2 + 1 < PAIRS and not P_SORT:
                         sort_p(done // 2 + 1)
-        for step in range(-AHEAD_NORM, N_STEPS + LAST + 12):
+        for step in range(-AHEAD_NORM, last_scaling + 1):
             if OUT_EARLY:
                 for group, k in out_steps.get(step + AHEAD_OUT, ()):
                     out_product(group, k)

from contextlib import ExitStack

import concourse.mybir as mybir
from concourse.masks import make_identity

F32 = mybir.dt.float32
BF16 = mybir.dt.bfloat16
U32 = mybir.dt.uint32
U8 = mybir.dt.uint8
FP8X4 = mybir.dt.float8_e4m3fn_x4
ACT = mybir.ActivationFunctionType
ALU = mybir.AluOpType

P = 128
B = 1024
K = 512
N_CAPS = 32
I = 16
J = 256
O = 16
COLS = J * O
B_TILES = B // P
G = N_CAPS // 2
BANK = 512
J_CHUNK = 128
J_PAIRS = J_CHUNK // 2
CHUNK = J_CHUNK * O
N_CHUNKS = J // J_CHUNK
O_TURN = 2
O_QUANT = 4
O_OUT = BANK // J_CHUNK

GROUP_TILES = 2
GROUP_ROWS = GROUP_TILES * P
O_NORM = BANK // GROUP_ROWS
GROUP_BANKS = 8
TILE_BANKS = GROUP_BANKS // GROUP_TILES
GROUP_Q = GROUP_TILES * J_CHUNK
GROUPS_PER_CHUNK = B_TILES // GROUP_TILES
N_GROUPS = N_CHUNKS * GROUPS_PER_CHUNK

COUPLING = 1.0 / 256.0
SQ_EPS = 1e-8
SHRINK = 2.0 ** -32

FLOPS = 2 * B * K * COLS


def tile_capsulenetwork_pb_kernel(tc, p, Wr, out):
    nc = tc.nc
    out_rows = out.rearrange("(r t) j o -> r t (j o)", t=B_TILES)

    with ExitStack() as ctx:
        keep = ctx.enter_context(tc.tile_pool(name="keep", bufs=1))
        stage = ctx.enter_context(tc.tile_pool(name="stage", bufs=2))
        quarters = ctx.enter_context(tc.tile_pool(name="quarters", bufs=4))
        squares_pool = ctx.enter_context(tc.tile_pool(name="squares_pool", bufs=16))
        pair_pool = ctx.enter_context(tc.tile_pool(name="pair_pool", bufs=2))
        work = ctx.enter_context(tc.tile_pool(name="work", bufs=3))
        results = ctx.enter_context(tc.tile_pool(name="results", bufs=4))
        copied_pool = ctx.enter_context(tc.tile_pool(name="copied_pool", bufs=2))
        psum_banks = ctx.enter_context(tc.psum_pool(name="psum_banks", bufs=7))
        psum_sums = ctx.enter_context(tc.psum_pool(name="psum_sums", bufs=1))

        p_raw = keep.tile([P, B_TILES, K], BF16)

        def load_p(pair):
            tiles = slice(2 * pair, 2 * pair + 2)
            nc.sync.dma_start(
                out=p_raw[:, tiles, :], in_=p.rearrange("(r t) n i -> r t (n i)", t=B_TILES)[:, tiles, :]
            )

        w_raws = []
        PIECES = 4
        G_PIECE = G // PIECES

        def load_w(c):
            w_raw = stage.tile([P, G, 2 * O * I], BF16)
            w_raws.append(w_raw)
            by_half = Wr[:, c * J_CHUNK : (c + 1) * J_CHUNK, :, :].rearrange(
                "(g u) (jp jl) o i -> u jp g (jl o i)", u=2, jl=2
            )
            for piece in range(PIECES):
                pairs = slice(piece * G_PIECE, (piece + 1) * G_PIECE)
                for u in range(2):
                    nc.sync.dma_start(out=w_raw[u:P:2, pairs, :], in_=by_half[u, :, pairs, :])

        P_AFTER = 0
        load_p(0)
        load_w(0)
        for pair in range(1, B_TILES // 2 - P_AFTER):
            load_p(pair)
        load_w(1)
        for pair in range(B_TILES // 2 - P_AFTER, B_TILES // 2):
            load_p(pair)

        shrink_col = keep.tile([P, 1], F32)
        nc.vector.memset(shrink_col[:], SHRINK)
        table_warmer = keep.tile([P, 1], F32)
        nc.scalar.activation(out=table_warmer[:], in_=shrink_col[:], func=ACT.Abs_reciprocal_sqrt)

        ident = keep.tile([P, P], F32)
        make_identity(nc, ident[:])

        p_codes = keep.tile([P, B_TILES * P], U32, align_bytes=64)
        p_scales = keep.tile([P, B_TILES * P], U8, align_bytes=64)
        w_codes = keep.tile([P, COLS], U32, align_bytes=64)
        w_scales = keep.tile([P, COLS], U8, align_bytes=64)

        def copy_out_of_psum(out_view, in_view, on_vector):
            if on_vector:
                nc.vector.tensor_copy(out=out_view, in_=in_view)
            else:
                nc.scalar.copy(out=out_view, in_=in_view)

        w_sorted = {}
        w_quarters = {}

        def sort_w(c, piece):
            if piece == 0:
                sorted_tile = stage.tile([P, 2 * O, G, I], BF16)
                w_sorted[c] = sorted_tile
            pairs = slice(piece * G_PIECE, (piece + 1) * G_PIECE)
            nc.vector.tensor_copy(
                out=w_sorted[c][:, :, pairs, :],
                in_=w_raws[c][:].rearrange("q g (lo i) -> q lo g i", i=I)[:, :, pairs, :],
            )

        turned_banks = {}

        def turn_w(c, bank):
            words = w_sorted[c][:].rearrange("q lo g i -> q lo (g i)").bitcast(F32)
            turned = psum_banks.tile([P, BANK], F32, tag="bank")
            for block in range(O_TURN * 2):
                o, jl = divmod(bank * O_TURN * 2 + block, 2)
                nc.tensor.transpose(turned[:, block * P : (block + 1) * P], words[:, jl * O + o, :], ident[:])
            turned_banks[(c, bank)] = turned

        def group_w(c, bank, on_vector):
            turned = turned_banks[(c, bank)]
            half = bank % 2
            if half == 0:
                quarter = quarters.tile([P, O_QUANT * J_CHUNK * 4], BF16, align_bytes=64)
                w_quarters[(c, bank // 2)] = quarter
            copy_out_of_psum(
                w_quarters[(c, bank // 2)][:].bitcast(F32)[:, half * BANK : (half + 1) * BANK], turned[:], on_vector
            )

        def quantise_w(c, quarter):
            first_col = c * CHUNK + quarter * O_QUANT * J_CHUNK
            cols = slice(first_col, first_col + O_QUANT * J_CHUNK)
            nc.vector.quantize_mx(
                out=w_codes[:, cols].bitcast(FP8X4),
                scales=w_scales[:, cols],
                in_=w_quarters[(c, quarter)][:],
            )

        p_sorted = keep.tile([P, B_TILES, 2, G, I], BF16)
        p_by_half = p_raw[:].rearrange("r t (g u i) -> r t g u i", u=2, i=I)

        def sort_p(pair):
            tiles = slice(2 * pair, 2 * pair + 2)
            for u in range(2):
                nc.vector.tensor_copy(out=p_sorted[:, tiles, u, :, :], in_=p_by_half[:, tiles, :, u, :])

        p_words = p_sorted[:].rearrange("r t u g i -> r (t u g i)").bitcast(F32)
        p_grouped = keep.tile([P, B_TILES * P * 4], BF16, align_bytes=64)
        p_grouped_words = p_grouped[:].bitcast(F32)

        def quantise_p(pair):
            nc.vector.quantize_mx(
                out=p_codes[:, pair * 2 * P : (pair + 1) * 2 * P].bitcast(FP8X4),
                scales=p_scales[:, pair * 2 * P : (pair + 1) * 2 * P],
                in_=p_grouped[:, pair * 2 * P * 4 : (pair + 1) * 2 * P * 4],
            )

        def turn_p(pair):
            turned = psum_banks.tile([P, BANK], F32, tag="bank")
            for tu in range(4):
                first_word = (pair * 4 + tu) * P
                nc.tensor.transpose(
                    turned[:, tu * P : (tu + 1) * P], p_words[:, first_word : first_word + P], ident[:]
                )
            turned_p[pair] = turned

        turned_p = {}

        def group_p(pair, on_vector):
            turned = turned_p[pair]
            copy_out_of_psum(
                p_grouped_words[:, pair * BANK : (pair + 1) * BANK].rearrange("m (t r u) -> m t r u", t=2, u=2),
                turned[:].rearrange("m (t u r) -> m t r u", t=2, u=2),
                on_vector,
            )

        pair_sums = {}
        summands = {}
        lengths = {}
        one_plus_sq = {}
        denom_sq = {}
        seeds = {}
        seeds_sq = {}
        roughs = {}
        x_y_sqs = {}
        factors = {}
        result = {}

        norm_banks = {}
        out_banks = {}

        def norm_product(group, k):
            first_row = (group % GROUPS_PER_CHUNK) * GROUP_ROWS
            acc = psum_banks.tile([P, O_NORM, GROUP_ROWS], F32, tag="bank")
            for ob in range(O_NORM):
                first_col = (group // GROUPS_PER_CHUNK) * CHUNK + (k * O_NORM + ob) * J_CHUNK
                nc.tensor.matmul_mx(
                    out=acc[:, ob, :],
                    lhsT=w_codes[:, first_col : first_col + P].bitcast(FP8X4),
                    lhsT_scale=w_scales[:, first_col : first_col + P],
                    rhs=p_codes[:, first_row : first_row + GROUP_ROWS].bitcast(FP8X4),
                    rhs_scale=p_scales[:, first_row : first_row + GROUP_ROWS],
                    start=True,
                    stop=True,
                )
            norm_banks[(group, k)] = acc

        def square_bank(group, k):
            acc = norm_banks[(group, k)]
            squares = squares_pool.tile([P, O_NORM, GROUP_ROWS], F32)
            nc.scalar.activation(out=squares[:], in_=acc[:], func=ACT.Square, scale=COUPLING)
            if k in (UNADDED_FIRST if group == 0 else UNADDED_LAST if group == N_GROUPS - 1 else UNADDED):
                summands.setdefault(group, []).extend([squares[:, ob, :] for ob in range(O_NORM)])
            else:
                if group not in pair_sums:
                    pair_tile = pair_pool.tile([P, GROUP_BANKS, GROUP_ROWS], F32)
                    pair_sums[group] = pair_tile
                pair_sum = pair_sums[group][:, k, :]
                nc.gpsimd.tensor_tensor(out=pair_sum, in0=squares[:, 0, :], in1=squares[:, 1, :], op=ALU.add)
                summands.setdefault(group, []).append(pair_sum)

        def sum_squares(group, tile_in_group):
            if tile_in_group == 0:
                q = psum_sums.tile([P, GROUP_TILES, J_CHUNK], F32, tag="sums")
                lengths[group] = q
            rows = slice(tile_in_group * P, (tile_in_group + 1) * P)
            for k, summand in enumerate(summands[group]):
                nc.tensor.matmul(
                    out=lengths[group][:, tile_in_group, :],
                    lhsT=summand[:, rows],
                    rhs=ident[:],
                    is_transpose=True,
                    start=(k == 0),
                    stop=(k == len(summands[group]) - 1),
                )

        def factor_one_plus_q(group):
            one_plus_q_sq = work.tile([P, GROUP_TILES, J_CHUNK], F32)
            nc.scalar.activation(
                out=one_plus_q_sq[:], in_=lengths[group][:], func=ACT.Square, scale=SHRINK, bias=shrink_col[:]
            )
            one_plus_sq[group] = one_plus_q_sq

        def factor_denominator(group):
            x = work.tile([P, GROUP_TILES, J_CHUNK], F32)
            nc.vector.scalar_tensor_tensor(
                out=x[:],
                in0=lengths[group][:],
                scalar=SQ_EPS,
                in1=one_plus_sq[group][:],
                op0=ALU.add,
                op1=ALU.mult,
            )
            denom_sq[group] = x

        def factor_seed(group):
            y = work.tile([P, GROUP_TILES, J_CHUNK], F32)
            nc.scalar.activation(out=y[:], in_=denom_sq[group][:], func=ACT.Abs_reciprocal_sqrt)
            seeds[group] = y

        def factor_seed_sq(group):
            y_sq = work.tile([P, GROUP_TILES, J_CHUNK], F32)
            nc.scalar.activation(out=y_sq[:], in_=seeds[group][:], func=ACT.Square)
            seeds_sq[group] = y_sq

        def factor_rough(group):
            rough = work.tile([P, GROUP_TILES, J_CHUNK], F32)
            nc.vector.scalar_tensor_tensor(
                out=rough[:],
                in0=lengths[group][:],
                scalar=-0.5 * SHRINK * COUPLING,
                in1=seeds[group][:],
                op0=ALU.mult,
                op1=ALU.mult,
            )
            roughs[group] = rough

        def factor_x_y_sq(group):
            x_y_sq = work.tile([P, GROUP_TILES, J_CHUNK], F32)
            nc.vector.tensor_tensor(out=x_y_sq[:], in0=denom_sq[group][:], in1=seeds_sq[group][:], op=ALU.mult)
            x_y_sqs[group] = x_y_sq

        def factor_newton(group):
            factor = work.tile([P, GROUP_TILES, J_CHUNK], F32)
            nc.vector.scalar_tensor_tensor(
                out=factor[:],
                in0=x_y_sqs[group][:],
                scalar=3.0,
                in1=roughs[group][:],
                op0=ALU.subtract,
                op1=ALU.mult,
            )
            factors[group] = factor

        def out_product(group, k):
            tile_in_group = k // 4
            quarter = k % 4
            t = GROUP_TILES * (group % GROUPS_PER_CHUNK) + tile_in_group
            c = group // GROUPS_PER_CHUNK
            first_col = c * CHUNK + quarter * BANK
            acc = psum_banks.tile([P, O_OUT, J_CHUNK], F32, tag="bank")
            nc.tensor.matmul_mx(
                out=acc[:].rearrange("r o j -> r (o j)"),
                lhsT=p_codes[:, t * P : (t + 1) * P].bitcast(FP8X4),
                lhsT_scale=p_scales[:, t * P : (t + 1) * P],
                rhs=w_codes[:, first_col : first_col + BANK].bitcast(FP8X4),
                rhs_scale=w_scales[:, first_col : first_col + BANK],
                start=True,
                stop=True,
            )
            out_banks[(group, k)] = acc

        copied_banks = {}
        unscaled = {}

        def copy_bank(group, k):
            copied = copied_pool.tile([P, 2, J_PAIRS, O_OUT], F32)
            nc.scalar.copy(out=copied[:], in_=out_banks[(group, k)][:].rearrange("r o (jl jp) -> r jl jp o", jl=2))
            copied_banks[(group, k)] = copied

        def scale_bank(group, k, half=None):
            tile_in_group, quarter = divmod(k, TILE_BANKS)
            t = GROUP_TILES * (group % GROUPS_PER_CHUNK) + tile_in_group
            c = group // GROUPS_PER_CHUNK
            if (group, tile_in_group) not in result:
                result_tile = results.tile([P, J_CHUNK, O], F32)
                result[(group, tile_in_group)] = result_tile
            n_j = J_CHUNK if half is None else J_CHUNK // 2
            first_j = 0 if half is None else half * n_j
            j = slice(first_j, first_j + n_j)
            jp = slice(first_j // 2, (first_j + n_j) // 2)
            aside = (group, k) in copied_banks
            bank = copied_banks[(group, k)][:] if aside else out_banks[(group, k)][:].rearrange("r o (jl jp) -> r jl jp o", jl=2)
            engine = nc.gpsimd if aside else nc.vector
            engine.tensor_tensor(
                out=result[(group, tile_in_group)][:].rearrange("r (jp jl) o -> r jl jp o", jl=2)[
                    :, :, jp, quarter * O_OUT : (quarter + 1) * O_OUT
                ],
                in0=bank[:, :, jp, :],
                in1=factors[group][:, tile_in_group, :]
                .rearrange("r (jl jp) -> r jl jp", jl=2)[:, :, jp]
                .unsqueeze(3)
                .to_broadcast([P, 2, n_j // 2, O_OUT]),
                op=ALU.mult,
            )
            part = (group, tile_in_group, half)
            unscaled[part] = unscaled.get(part, TILE_BANKS) - 1
            if unscaled[part] == 0:
                first_col = c * CHUNK + first_j * O
                nc.sync.dma_start(
                    out=out_rows[:, t, first_col : first_col + n_j * O],
                    in_=result[(group, tile_in_group)][:, j, :].rearrange("r j o -> r (j o)"),
                )

        AHEAD_NORM = 2
        AHEAD_OUT = 2
        LAGS = (1, 2, 4, 5, 6, 7, 8, 9, 9)
        LAGS_FIRST = (1, 3, 5, 5, 7, 7, 8, 8, 10)
        LAGS_LAST = (2, 3, 3, 4, 5, 6, 6, 7, 8)
        UNADDED_FIRST = (0, 1, 2, 3, 4, 5, 6, 7)
        UNADDED = (7,)
        UNADDED_LAST = (7,)
        P_MERGE = 1
        P_SORT = 1
        W1_QUANT = 3
        W1_ON_V = (1, 3, 5, 7)
        W1_SORT_EVERY = 1
        HEAD_V = (1, 4, 7)
        SUMS_END = 0
        OUT_EARLY = 0
        LAST = GROUP_BANKS - 1
        N_STEPS = N_GROUPS * GROUP_BANKS
        PAIRS = B_TILES // 2
        N_TURNS = O // O_TURN
        P_TURN = 2
        W1_SORT = 1
        W1_TURN = 6
        W1_EVERY = 3
        ctx.enter_context(tc.manual_schedule())
        sort_p(0)
        turn_p(0)
        group_p(0, on_vector=False)
        warm_up = psum_sums.tile([P, BANK], F32, tag="sums")

        def keep_warm(piece):
            for n in range(piece * G_PIECE, piece * G_PIECE + WARM_MATMULS):
                nc.tensor.matmul(
                    out=warm_up[:],
                    lhsT=p_raw[:, 0, :P],
                    rhs=w_raws[0][:, n, :],
                    start=True,
                    stop=True,
                )

        WARM_MATMULS = 3
        for piece in range(PIECES):
            sort_w(0, piece)
            if piece in (1, 2):
                keep_warm(piece)
            if piece == 1:
                quantise_p(0)
        ASIDE_LIST = ((6, 0), (6, 1))
        ASIDE = ASIDE_LIST
        out_steps = {}
        out_step = 0
        for group in range(N_GROUPS):
            lags = LAGS_FIRST if group == 0 else LAGS_LAST if group == N_GROUPS - 1 else LAGS
            out_step = max(out_step, group * GROUP_BANKS + LAST + lags[-1])
            for k in range(GROUP_BANKS):
                out_steps.setdefault(out_step, []).append((group, k))
                if (group, k) not in ASIDE:
                    out_step += 1
        last_scaling = out_step - 1
        HEAD = 3
        if P_SORT:
            for pair in range(1, PAIRS):
                sort_p(pair)
        for bank in range(N_TURNS + HEAD):
            if bank < N_TURNS:
                turn_w(0, bank)
            done = bank - HEAD
            if done >= 0:
                group_w(0, done, on_vector=(done in HEAD_V))
                if done % 2 == 1:
                    quantise_w(0, done // 2)
                    if done // 2 + 1 < PAIRS and not P_SORT:
                        sort_p(done // 2 + 1)
        for step in range(-AHEAD_NORM, last_scaling + 1):
            if OUT_EARLY:
                for group, k in out_steps.get(step + AHEAD_OUT, ()):
                    out_product(group, k)
                    if (group, k) in ASIDE:
                        copy_bank(group, k)
            ahead = step + AHEAD_NORM
            if ahead < N_STEPS:
                norm_product(ahead // GROUP_BANKS, ahead % GROUP_BANKS)
            if 0 <= step < N_STEPS:
                square_bank(step // GROUP_BANKS, step % GROUP_BANKS)
            for pair in range(1, PAIRS):
                turn_step = P_TURN + (0 if P_MERGE else pair - 1)
                if step == turn_step:
                    turn_p(pair)
            for pair in range(1, PAIRS):
                if step == P_TURN + pair:
                    group_p(pair, on_vector=False)
                if step == P_TURN + pair + 1:
                    quantise_p(pair)
            for piece in range(PIECES):
                if step == W1_SORT + piece * W1_SORT_EVERY:
                    sort_w(1, piece)
            for turns in range(N_TURNS // 2):
                if step == W1_TURN + turns * W1_EVERY:
                    turn_w(1, 2 * turns)
                    turn_w(1, 2 * turns + 1)
                if step == W1_TURN + turns * W1_EVERY + 1:
                    group_w(1, 2 * turns, 2 * turns in W1_ON_V)
                    group_w(1, 2 * turns + 1, 2 * turns + 1 in W1_ON_V)
                if step == W1_TURN + turns * W1_EVERY + W1_QUANT:
                    quantise_w(1, turns)
            group, offset = divmod(step - LAST, GROUP_BANKS)
            for late in (0, 1):
                for back in range(3):
                    g, off = group - back, offset + back * GROUP_BANKS
                    if 0 <= g < N_GROUPS:
                        lags = LAGS_FIRST if g == 0 else LAGS_LAST if g == N_GROUPS - 1 else LAGS
                        actions = (
                            factor_one_plus_q,
                            factor_denominator,
                            factor_seed,
                            factor_seed_sq,
                            factor_rough,
                            factor_x_y_sq,
                            factor_newton,
                        )
                        if late == SUMS_END:
                            for tile_in_group in range(GROUP_TILES):
                                if off == lags[tile_in_group]:
                                    sum_squares(g, tile_in_group)
                        if late == 0:
                            for lag, action in zip(lags[GROUP_TILES:], actions):
                                if off == lag:
                                    action(g)
            if not OUT_EARLY:
                for group, k in out_steps.get(step + AHEAD_OUT, ()):
                    out_product(group, k)
                    if (group, k) in ASIDE:
                        copy_bank(group, k)
            for group, k in out_steps.get(step, ()):
                if group < N_GROUPS - 1 or k < GROUP_BANKS - TILE_BANKS:
                    scale_bank(group, k)
            if step == last_scaling:
                for half in range(2):
                    for k in range(GROUP_BANKS - TILE_BANKS, GROUP_BANKS):
                        scale_bank(N_GROUPS - 1, k, half)
